import numpy as np
import ml_dtypes


def mxq(x, axis, fmt="e4m3"):
    dtype, down = {"e4m3": (ml_dtypes.float8_e4m3fn, 7), "e5m2": (ml_dtypes.float8_e5m2, 14)}[fmt]
    v = np.moveaxis(np.asarray(x, np.float32).astype(ml_dtypes.bfloat16).astype(np.float64), axis, -1)
    blocks = v.reshape(v.shape[:-1] + (-1, 32))
    amax = np.abs(blocks).max(-1, keepdims=True)
    byte = np.maximum(np.where(amax > 0, np.frexp(amax)[1] - 1 + 127, 0) - down, 1)
    scale = np.exp2(byte - 127.0)
    codes = (blocks / scale).astype(np.float32).astype(dtype).astype(np.float64)
    return np.moveaxis((codes * scale).reshape(v.shape), -1, axis)


WIDE = False


def mx_kscale(k):
    if not WIDE:
        return np.ones(k)
    levels = np.array([20, -20, 10, -10, 0])
    a = np.random.permutation(np.resize(levels, k // 512 * 4)).reshape(k // 512, 4)
    idx = np.arange(k)
    return np.exp2(a[idx // 512, idx % 128 // 32])


BF16 = ml_dtypes.bfloat16


def bf(x):
    return np.asarray(x, np.float32).astype(BF16)


def f64(x):
    return np.asarray(x).astype(np.float64)


B, T, D, NH, HD, G, RD, F = 1, 1024, 1024, 8, 128, 2, 16, 4096
HKV = NH // G
C = NH * HD


def setup_inputs():
    u = mx_kscale(D)
    v = np.random.standard_normal((B, HKV, T, HD))
    a = 0.4 * np.random.standard_normal((B, HKV, G, T, HD)) + 0.4 * v[:, :, None]
    x = np.random.standard_normal((B, T, D)) * np.random.uniform(0.5, 2.0, (B, T, 1))
    wo = np.random.standard_normal((D, C)) / np.sqrt(C) / u[:, None]
    sc = 1.0 + 0.1 * np.random.standard_normal(D)
    g = 4.0 * np.random.standard_normal((B, T, D)) * np.exp2(np.random.randint(-12, 1, (B, T, 1))) * u
    return {"attn_out": bf(a),
            "v": bf(v),
            "x": bf(x),
            "wo": bf(wo),
            "attn_scale": bf(sc),
            "grad_out": bf(g)}


def reference(attn_out, v, x, wo, attn_scale, grad_out):
    gs = f64(grad_out) * f64(attn_scale)
    gy = mxq(gs, 2, "e5m2") @ mxq(f64(wo), 0, "e4m3")
    gy = gy.reshape(B, T, HKV, G, HD)
    v_t = f64(v).transpose(0, 2, 1, 3)
    vn = v_t / np.maximum(np.sqrt(np.sum(np.square(v_t), axis=-1, keepdims=True)), 1e-12)
    vn = vn[:, :, :, None, :]
    ga = gy - np.sum(gy * vn, axis=-1, keepdims=True) * vn
    return ga.transpose(0, 2, 3, 1, 4)

@@ -1,0 +1,175 @@
+from contextlib import ExitStack
+
+import concourse.masks as masks
+import concourse.mybir as mybir
+
+F32 = mybir.dt.float32
+BF16 = mybir.dt.bfloat16
+U32 = mybir.dt.uint32
+U8 = mybir.dt.uint8
+E4M3X4 = mybir.dt.float8_e4m3fn_x4
+E5M2X4 = mybir.dt.float8_e5m2_x4
+ALU = mybir.AluOpType
+ACT = mybir.ActivationFunctionType
+
+P = 128
+T = 1024
+D = 1024
+HKV = 4
+HD = 128
+C = 1024
+PASSES = D // 512
+TILES = T // P
+PAIRS = TILES // 2
+N = 512
+HALVES = C // N
+HEADS_PER_HALF = N // HD
+
+FLOPS = 2 * T * D * C
+BYTES = 2 * (T * D + D * C + HKV * T * HD + D) + 4 * T * C
+
+
+def tile_block_pb_kernel(tc, attn_out, v, x, wo, attn_scale, grad_out, out):
+    nc = tc.nc
+    go_view = grad_out.rearrange("b (p i) d -> p (b i) d", i=TILES)
+    v_view = v.rearrange("b h (p i) d -> p (b h) i d", i=TILES)
+    out_view = out.rearrange("b h g (p i) d -> p (b h g) i d", i=TILES)
+
+    with ExitStack() as ctx:
+        keep = ctx.enter_context(tc.tile_pool(name="keep", bufs=1))
+        work = ctx.enter_context(tc.tile_pool(name="work", bufs=4))
+        results = ctx.enter_context(tc.tile_pool(name="results", bufs=3))
+        psum_xt = ctx.enter_context(tc.psum_pool(name="psum_xt", bufs=2))
+        psum_gy = ctx.enter_context(tc.psum_pool(name="psum_gy", bufs=6))
+
+        ident = keep.tile([P, P], F32)
+        sc = keep.tile([P, PASSES, 2, 2], BF16)
+        go_sb = keep.tile([P, TILES, D], BF16)
+        wo_raw = keep.tile([P, PASSES, 4, C], BF16)
+        wo_grp = keep.tile([P, PASSES, C, 4], BF16, align_bytes=64)
+        wo_codes = keep.tile([P, PASSES, C], U32, align_bytes=64)
+        wo_scales = keep.tile([P, PASSES, C], U8, align_bytes=64)
+        gs_grp = keep.tile([P, TILES, PASSES, P, 2, 2], BF16, align_bytes=64)
+        gs_codes = keep.tile([P, TILES, PASSES, P], U32, align_bytes=64)
+        gs_scales = keep.tile([P, TILES, PASSES, P], U8, align_bytes=64)
+        v_sb = keep.tile([P, HKV, TILES, HD], BF16)
+        v_squares = keep.tile([P, TILES, HKV, HD], BF16)
+        ss = keep.tile([P, TILES, HKV], F32)
+        nq = keep.tile([P, TILES, HKV], F32)
+        warm = keep.tile([P, 1], F32)
+
+        masks.make_identity(nc, ident[:])
+        nc.scalar.activation(out=warm[:], in_=ident[:, 0:1], func=ACT.Square)
+
+        with nc.allow_non_contiguous_dma(reason="1024 scale values, two to a piece"):
+            nc.scalar.dma_start(
+                out=sc[:].rearrange("p g u e -> p (g u) e"),
+                in_=attn_scale.rearrange("(a p e) -> p a e", p=P, e=2),
+            )
+
+        def load_go(j):
+            nc.sync.dma_start(out=go_sb[:, 2 * j : 2 * j + 2, :], in_=go_view[:, 2 * j : 2 * j + 2, :])
+
+        def load_wo(g):
+            nc.sync.dma_start(
+                out=wo_raw[:, g].rearrange("p (u e) c -> p u (e c)", e=2),
+                in_=wo[512 * g : 512 * (g + 1), :].rearrange("(u p e) c -> p u (e c)", p=P, e=2),
+            )
+
+        load_go(0)
+        load_wo(0)
+        load_go(1)
+        load_wo(1)
+        load_go(2)
+        nc.sync.dma_start(out=v_sb[:], in_=v_view)
+        load_go(3)
+
+        for j in range(PAIRS):
+            for i in (2 * j, 2 * j + 1):
+                go_words = go_sb[:, i, :].bitcast(F32)
+                xt = psum_xt.tile([P, 4 * P], F32)
+                for a in range(4):
+                    nc.tensor.transpose(xt[:, a * P : (a + 1) * P], go_words[:, a * P : (a + 1) * P], ident[:])
+                halves = xt[:].bitcast(BF16).rearrange("p (g u r e) -> p g r u e", g=PASSES, u=2, e=2)
+                for g in range(PASSES):
+                    nc.vector.tensor_tensor(
+                        out=gs_grp[:, i, g],
+                        in0=halves[:, g],
+                        in1=sc[:, g].unsqueeze(1).to_broadcast([P, P, 2, 2]),
+                        op=ALU.mult,
+                    )
+            nc.vector.quantize_mx(
+                out=gs_codes[:, 2 * j : 2 * j + 2].rearrange("p i g r -> p (i g r)").bitcast(E5M2X4),
+                scales=gs_scales[:, 2 * j : 2 * j + 2].rearrange("p i g r -> p (i g r)"),
+                in_=gs_grp[:, 2 * j : 2 * j + 2].rearrange("p i g r u e -> p (i g r u e)"),
+            )
+            g, n = divmod(j, HALVES)
+            cols = slice(n * N, (n + 1) * N)
+            nc.scalar.copy(
+                out=wo_grp[:, g, cols, :].rearrange("p (c i) t -> p c t i", i=4),
+                in_=wo_raw[:, g, :, cols].rearrange("p t (c i) -> p c t i", i=4),
+            )
+            nc.vector.quantize_mx(
+                out=wo_codes[:, g, cols].bitcast(E4M3X4),
+                scales=wo_scales[:, g, cols],
+                in_=wo_grp[:, g, cols, :].rearrange("p c t -> p (c t)"),
+            )
+
+        for j in range(PAIRS):
+            for i in (2 * j, 2 * j + 1):
+                for h in range(HKV):
+                    nc.scalar.activation(
+                        out=v_squares[:, i, h, :], in_=v_sb[:, h, i, :], func=ACT.Square, accum_out=ss[:, i, h : h + 1]
+                    )
+            pair = slice(2 * j, 2 * j + 2)
+            nc.vector.tensor_scalar(
+                out=nq[:, pair, :], in0=ss[:, pair, :], scalar1=1e-24, scalar2=-1.0, op0=ALU.max, op1=ALU.mult
+            )
+            nc.vector.reciprocal(out=nq[:, pair, :], in_=nq[:, pair, :])
+
+        for j in range(PAIRS):
+            for n in range(HALVES):
+                cols = slice(n * N, (n + 1) * N)
+                res = results.tile([P, HEADS_PER_HALF, 2, HD], F32)
+                for i2 in range(2):
+                    i = 2 * j + i2
+                    gy = psum_gy.tile([P, HEADS_PER_HALF, HD], F32)
+                    for g in range(PASSES):
+                        nc.tensor.matmul_mx(
+                            out=gy[:].rearrange("p q d -> p (q d)"),
+                            lhsT=gs_codes[:, i, g, :].bitcast(E5M2X4),
+                            lhsT_scale=gs_scales[:, i, g, :],
+                            rhs=wo_codes[:, g, cols].bitcast(E4M3X4),
+                            rhs_scale=wo_scales[:, g, cols],
+                            start=(g == 0),
+                            stop=(g == PASSES - 1),
+                        )
+                    prod = work.tile([P, HEADS_PER_HALF, HD], F32)
+                    for h2 in range(2):
+                        h = 2 * n + h2
+                        nc.vector.scalar_tensor_tensor(
+                            out=prod[:, 2 * h2 : 2 * h2 + 2, :],
+                            in0=gy[:, 2 * h2 : 2 * h2 + 2, :],
+                            scalar=nq[:, i, h : h + 1],
+                            in1=v_sb[:, h, i, :].unsqueeze(1).to_broadcast([P, 2, HD]),
+                            op0=ALU.mult,
+                            op1=ALU.mult,
+                        )
+                    negc = work.tile([P, HEADS_PER_HALF], F32)
+                    unread = work.tile([P, HEADS_PER_HALF, HD], BF16)
+                    for q in range(HEADS_PER_HALF):
+                        nc.scalar.activation(
+                            out=unread[:, q, :], in_=prod[:, q, :], func=ACT.Copy, accum_out=negc[:, q : q + 1]
+                        )
+                    for q in range(HEADS_PER_HALF):
+                        nc.vector.scalar_tensor_tensor(
+                            out=res[:, q, i2, :],
+                            in0=v_sb[:, 2 * n + q // 2, i, :],
+                            scalar=negc[:, q : q + 1],
+                            in1=gy[:, q, :],
+                            op0=ALU.mult,
+                            op1=ALU.add,
+                        )
+                nc.sync.dma_start(
+                    out=out_view[:, n * HEADS_PER_HALF : (n + 1) * HEADS_PER_HALF, 2 * j : 2 * j + 2, :], in_=res[:]
+                )

@@ -24,6 +24,10 @@ PAIRS = TILES // 2
 N = 512
 HALVES = C // N
 HEADS_PER_HALF = N // HD
+UNITS = TILES * HALVES
+DOT_LAG = 2
+FINISH_LAG = 3
+ON_GPSIMD = (2, 4, 6, 8, 10, 12)
 
 FLOPS = 2 * T * D * C
 BYTES = 2 * (T * D + D * C + HKV * T * HD + D) + 4 * T * C
@@ -38,9 +42,8 @@ def tile_block_pb_kernel(tc, attn_out, v, x, wo, attn_scale, grad_out, out):
     with ExitStack() as ctx:
         keep = ctx.enter_context(tc.tile_pool(name="keep", bufs=1))
         work = ctx.enter_context(tc.tile_pool(name="work", bufs=4))
-        results = ctx.enter_context(tc.tile_pool(name="results", bufs=3))
-        psum_xt = ctx.enter_context(tc.psum_pool(name="psum_xt", bufs=2))
-        psum_gy = ctx.enter_context(tc.psum_pool(name="psum_gy", bufs=6))
+        results = ctx.enter_context(tc.tile_pool(name="results", bufs=4))
+        psum = ctx.enter_context(tc.psum_pool(name="psum", bufs=8))
 
         ident = keep.tile([P, P], F32)
         sc = keep.tile([P, PASSES, 2, 2], BF16)
@@ -53,8 +56,8 @@ def tile_block_pb_kernel(tc, attn_out, v, x, wo, attn_scale, grad_out, out):
         gs_codes = keep.tile([P, TILES, PASSES, P], U32, align_bytes=64)
         gs_scales = keep.tile([P, TILES, PASSES, P], U8, align_bytes=64)
         v_sb = keep.tile([P, HKV, TILES, HD], BF16)
-        v_squares = keep.tile([P, TILES, HKV, HD], BF16)
         ss = keep.tile([P, TILES, HKV], F32)
+        clamped = keep.tile([P, TILES, HKV], F32)
         nq = keep.tile([P, TILES, HKV], F32)
         warm = keep.tile([P, 1], F32)
 
@@ -62,13 +65,14 @@ def tile_block_pb_kernel(tc, attn_out, v, x, wo, attn_scale, grad_out, out):
         nc.scalar.activation(out=warm[:], in_=ident[:, 0:1], func=ACT.Square)
 
         with nc.allow_non_contiguous_dma(reason="1024 scale values, two to a piece"):
-            nc.scalar.dma_start(
+            nc.sync.dma_start(
                 out=sc[:].rearrange("p g u e -> p (g u) e"),
                 in_=attn_scale.rearrange("(a p e) -> p a e", p=P, e=2),
             )
 
-        def load_go(j):
-            nc.sync.dma_start(out=go_sb[:, 2 * j : 2 * j + 2, :], in_=go_view[:, 2 * j : 2 * j + 2, :])
+        def load_go(first, count):
+            tiles = slice(first, first + count)
+            nc.sync.dma_start(out=go_sb[:, tiles, :], in_=go_view[:, tiles, :])
 
         def load_wo(g):
             nc.sync.dma_start(
@@ -76,100 +80,173 @@ def tile_block_pb_kernel(tc, attn_out, v, x, wo, attn_scale, grad_out, out):
                 in_=wo[512 * g : 512 * (g + 1), :].rearrange("(u p e) c -> p u (e c)", p=P, e=2),
             )
 
-        load_go(0)
+        load_go(0, 1)
+        load_go(1, 1)
         load_wo(0)
-        load_go(1)
         load_wo(1)
-        load_go(2)
         nc.sync.dma_start(out=v_sb[:], in_=v_view)
-        load_go(3)
+        load_go(2, 2)
+        load_go(4, 2)
+        load_go(6, 2)
 
-        for j in range(PAIRS):
-            for i in (2 * j, 2 * j + 1):
-                go_words = go_sb[:, i, :].bitcast(F32)
-                xt = psum_xt.tile([P, 4 * P], F32)
-                for a in range(4):
-                    nc.tensor.transpose(xt[:, a * P : (a + 1) * P], go_words[:, a * P : (a + 1) * P], ident[:])
-                halves = xt[:].bitcast(BF16).rearrange("p (g u r e) -> p g r u e", g=PASSES, u=2, e=2)
-                for g in range(PASSES):
-                    nc.vector.tensor_tensor(
-                        out=gs_grp[:, i, g],
-                        in0=halves[:, g],
-                        in1=sc[:, g].unsqueeze(1).to_broadcast([P, P, 2, 2]),
-                        op=ALU.mult,
-                    )
+        def transpose_and_scale(i):
+            go_words = go_sb[:, i, :].bitcast(F32)
+            bank = psum.tile([P, N], F32)
+            for a in range(4):
+                nc.tensor.transpose(bank[:, a * P : (a + 1) * P], go_words[:, a * P : (a + 1) * P], ident[:])
+            halves = bank[:].bitcast(BF16).rearrange("p (g u r e) -> p g r u e", g=PASSES, u=2, e=2)
+            for g in range(PASSES):
+                nc.vector.tensor_tensor(
+                    out=gs_grp[:, i, g],
+                    in0=halves[:, g],
+                    in1=sc[:, g].unsqueeze(1).to_broadcast([P, P, 2, 2]),
+                    op=ALU.mult,
+                )
+
+        def quantize_gs(j):
             nc.vector.quantize_mx(
                 out=gs_codes[:, 2 * j : 2 * j + 2].rearrange("p i g r -> p (i g r)").bitcast(E5M2X4),
                 scales=gs_scales[:, 2 * j : 2 * j + 2].rearrange("p i g r -> p (i g r)"),
                 in_=gs_grp[:, 2 * j : 2 * j + 2].rearrange("p i g r u e -> p (i g r u e)"),
             )
-            g, n = divmod(j, HALVES)
+
+        def regroup_wo(copy, g, n):
             cols = slice(n * N, (n + 1) * N)
-            nc.scalar.copy(
+            copy(
                 out=wo_grp[:, g, cols, :].rearrange("p (c i) t -> p c t i", i=4),
                 in_=wo_raw[:, g, :, cols].rearrange("p t (c i) -> p c t i", i=4),
             )
+
+        def quantize_wo(g, n):
+            cols = slice(n * N, (n + 1) * N)
             nc.vector.quantize_mx(
                 out=wo_codes[:, g, cols].bitcast(E4M3X4),
                 scales=wo_scales[:, g, cols],
                 in_=wo_grp[:, g, cols, :].rearrange("p c t -> p (c t)"),
             )
 
-        for j in range(PAIRS):
+        def norms(j):
             for i in (2 * j, 2 * j + 1):
                 for h in range(HKV):
+                    squares = work.tile([P, HD], BF16)
                     nc.scalar.activation(
-                        out=v_squares[:, i, h, :], in_=v_sb[:, h, i, :], func=ACT.Square, accum_out=ss[:, i, h : h + 1]
+                        out=squares[:], in_=v_sb[:, h, i, :], func=ACT.Square, accum_out=ss[:, i, h : h + 1]
                     )
             pair = slice(2 * j, 2 * j + 2)
-            nc.vector.tensor_scalar(
-                out=nq[:, pair, :], in0=ss[:, pair, :], scalar1=1e-24, scalar2=-1.0, op0=ALU.max, op1=ALU.mult
+            nc.gpsimd.tensor_scalar(
+                out=clamped[:, pair, :], in0=ss[:, pair, :], scalar1=1e-24, scalar2=-1.0, op0=ALU.max, op1=ALU.mult
             )
-            nc.vector.reciprocal(out=nq[:, pair, :], in_=nq[:, pair, :])
 
-        for j in range(PAIRS):
-            for n in range(HALVES):
-                cols = slice(n * N, (n + 1) * N)
+        def invert_norms(j):
+            pair = slice(2 * j, 2 * j + 2)
+            nc.vector.reciprocal(out=nq[:, pair, :], in_=clamped[:, pair, :])
+
+        def place(k):
+            j, n, i2 = k // 4, k // 2 % 2, k % 2
+            return j, n, i2, 2 * j + i2
+
+        gys, prods, negcs, ress = {}, {}, {}, {}
+
+        def multiply(k):
+            j, n, i2, i = place(k)
+            cols = slice(n * N, (n + 1) * N)
+            bank = psum.tile([P, N], F32)
+            for g in range(PASSES):
+                nc.tensor.matmul_mx(
+                    out=bank[:],
+                    lhsT=gs_codes[:, i, g, :].bitcast(E5M2X4),
+                    lhsT_scale=gs_scales[:, i, g, :],
+                    rhs=wo_codes[:, g, cols].bitcast(E4M3X4),
+                    rhs_scale=wo_scales[:, g, cols],
+                    start=(g == 0),
+                    stop=(g == PASSES - 1),
+                )
+            gys[k] = bank
+
+        def product(k):
+            j, n, i2, i = place(k)
+            v_pair = v_sb[:, 2 * n : 2 * n + 2, i, :].unsqueeze(2).to_broadcast([P, 2, 2, HD])
+            prod = work.tile([P, HEADS_PER_HALF, HD], F32)
+            prod_view = prod[:].rearrange("p (h q) d -> p h q d", q=2)
+            if k in ON_GPSIMD:
+                gy_sb = work.tile([P, N], F32)
+                nc.scalar.copy(out=gy_sb[:], in_=gys[k][:])
+                nc.gpsimd.tensor_tensor(
+                    out=prod_view, in0=gy_sb[:].rearrange("p (h q d) -> p h q d", h=2, q=2), in1=v_pair, op=ALU.mult
+                )
+            else:
+                nc.vector.tensor_tensor(
+                    out=prod_view, in0=gys[k][:].rearrange("p (h q d) -> p h q d", h=2, q=2), in1=v_pair, op=ALU.mult
+                )
+            prods[k] = prod
+
+        def dots(k):
+            j, n, i2, i = place(k)
+            negc = work.tile([P, HEADS_PER_HALF], F32)
+            for q in range(HEADS_PER_HALF):
+                h = 2 * n + q // 2
+                unread = work.tile([P, HD], BF16)
+                nc.scalar.activation(
+                    out=unread[:],
+                    in_=prods[k][:, q, :],
+                    func=ACT.Copy,
+                    scale=nq[:, i, h : h + 1],
+                    accum_out=negc[:, q : q + 1],
+                )
+            negcs[k] = negc
+
+        def finish(k):
+            j, n, i2, i = place(k)
+            if i2 == 0:
                 res = results.tile([P, HEADS_PER_HALF, 2, HD], F32)
-                for i2 in range(2):
-                    i = 2 * j + i2
-                    gy = psum_gy.tile([P, HEADS_PER_HALF, HD], F32)
-                    for g in range(PASSES):
-                        nc.tensor.matmul_mx(
-                            out=gy[:].rearrange("p q d -> p (q d)"),
-                            lhsT=gs_codes[:, i, g, :].bitcast(E5M2X4),
-                            lhsT_scale=gs_scales[:, i, g, :],
-                            rhs=wo_codes[:, g, cols].bitcast(E4M3X4),
-                            rhs_scale=wo_scales[:, g, cols],
-                            start=(g == 0),
-                            stop=(g == PASSES - 1),
-                        )
-                    prod = work.tile([P, HEADS_PER_HALF, HD], F32)
-                    for h2 in range(2):
-                        h = 2 * n + h2
-                        nc.vector.scalar_tensor_tensor(
-                            out=prod[:, 2 * h2 : 2 * h2 + 2, :],
-                            in0=gy[:, 2 * h2 : 2 * h2 + 2, :],
-                            scalar=nq[:, i, h : h + 1],
-                            in1=v_sb[:, h, i, :].unsqueeze(1).to_broadcast([P, 2, HD]),
-                            op0=ALU.mult,
-                            op1=ALU.mult,
-                        )
-                    negc = work.tile([P, HEADS_PER_HALF], F32)
-                    unread = work.tile([P, HEADS_PER_HALF, HD], BF16)
-                    for q in range(HEADS_PER_HALF):
-                        nc.scalar.activation(
-                            out=unread[:, q, :], in_=prod[:, q, :], func=ACT.Copy, accum_out=negc[:, q : q + 1]
-                        )
-                    for q in range(HEADS_PER_HALF):
-                        nc.vector.scalar_tensor_tensor(
-                            out=res[:, q, i2, :],
-                            in0=v_sb[:, 2 * n + q // 2, i, :],
-                            scalar=negc[:, q : q + 1],
-                            in1=gy[:, q, :],
-                            op0=ALU.mult,
-                            op1=ALU.add,
-                        )
+                ress[k // 2] = res
+            res = ress[k // 2]
+            for q in range(HEADS_PER_HALF):
+                nc.vector.scalar_tensor_tensor(
+                    out=res[:, q, i2, :],
+                    in0=v_sb[:, 2 * n + q // 2, i, :],
+                    scalar=negcs[k][:, q : q + 1],
+                    in1=gys[k][:, q * HD : (q + 1) * HD],
+                    op0=ALU.mult,
+                    op1=ALU.add,
+                )
+            if i2 == 1:
                 nc.sync.dma_start(
                     out=out_view[:, n * HEADS_PER_HALF : (n + 1) * HEADS_PER_HALF, 2 * j : 2 * j + 2, :], in_=res[:]
                 )
+
+        ctx.enter_context(tc.manual_schedule())
+        transpose_and_scale(0)
+        transpose_and_scale(1)
+        quantize_gs(0)
+        regroup_wo(nc.scalar.copy, 0, 0)
+        regroup_wo(nc.vector.tensor_copy, 0, 1)
+        quantize_wo(0, 1)
+        quantize_wo(0, 0)
+        regroup_wo(nc.scalar.copy, 1, 0)
+        regroup_wo(nc.vector.tensor_copy, 1, 1)
+        quantize_wo(1, 1)
+        quantize_wo(1, 0)
+        norms(0)
+        norms(1)
+        for k in range(UNITS + FINISH_LAG):
+            if k < UNITS:
+                multiply(k)
+                product(k)
+            if k == 1:
+                invert_norms(0)
+            if k in (1, 4, 6):
+                j = max(k // 2, 1)
+                transpose_and_scale(2 * j)
+                transpose_and_scale(2 * j + 1)
+            if k in (2, 5, 7):
+                j = k // 2
+                quantize_gs(j)
+            if k in (4, 7, 10):
+                invert_norms(k // 3)
+            if DOT_LAG <= k < UNITS + DOT_LAG:
+                dots(k - DOT_LAG)
+            if k in (4, 7):
+                norms(k // 2 if k == 4 else 3)
+            if FINISH_LAG <= k:
+                finish(k - FINISH_LAG)

@@ -25,9 +25,10 @@ N = 512
 HALVES = C // N
 HEADS_PER_HALF = N // HD
 UNITS = TILES * HALVES
-DOT_LAG = 2
-FINISH_LAG = 3
-ON_GPSIMD = (2, 4, 6, 8, 10, 12)
+DOT_LAG = 3
+FINISH_LAG = 4
+GPSIMD_LAG = 3
+ON_GPSIMD = (1, 4, 8)
 
 FLOPS = 2 * T * D * C
 BYTES = 2 * (T * D + D * C + HKV * T * HD + D) + 4 * T * C
@@ -41,8 +42,8 @@ def tile_block_pb_kernel(tc, attn_out, v, x, wo, attn_scale, grad_out, out):
 
     with ExitStack() as ctx:
         keep = ctx.enter_context(tc.tile_pool(name="keep", bufs=1))
-        work = ctx.enter_context(tc.tile_pool(name="work", bufs=4))
-        results = ctx.enter_context(tc.tile_pool(name="results", bufs=4))
+        work = ctx.enter_context(tc.tile_pool(name="work", bufs=6))
+        results = ctx.enter_context(tc.tile_pool(name="results", bufs=6))
         psum = ctx.enter_context(tc.psum_pool(name="psum", bufs=8))
 
         ident = keep.tile([P, P], F32)
@@ -84,8 +85,8 @@ def tile_block_pb_kernel(tc, attn_out, v, x, wo, attn_scale, grad_out, out):
         load_go(1, 1)
         load_wo(0)
         load_wo(1)
-        nc.sync.dma_start(out=v_sb[:], in_=v_view)
         load_go(2, 2)
+        nc.sync.dma_start(out=v_sb[:], in_=v_view)
         load_go(4, 2)
         load_go(6, 2)
 
@@ -145,7 +146,8 @@ def tile_block_pb_kernel(tc, attn_out, v, x, wo, attn_scale, grad_out, out):
             j, n, i2 = k // 4, k // 2 % 2, k % 2
             return j, n, i2, 2 * j + i2
 
-        gys, prods, negcs, ress = {}, {}, {}, {}
+        gys, gy_copies, prods, negcs, ress = {}, {}, {}, {}, {}
+        finished = set()
 
         def multiply(k):
             j, n, i2, i = place(k)
@@ -171,6 +173,7 @@ def tile_block_pb_kernel(tc, attn_out, v, x, wo, attn_scale, grad_out, out):
             if k in ON_GPSIMD:
                 gy_sb = work.tile([P, N], F32)
                 nc.scalar.copy(out=gy_sb[:], in_=gys[k][:])
+                gy_copies[k] = gy_sb
                 nc.gpsimd.tensor_tensor(
                     out=prod_view, in0=gy_sb[:].rearrange("p (h q d) -> p h q d", h=2, q=2), in1=v_pair, op=ALU.mult
                 )
@@ -197,23 +200,40 @@ def tile_block_pb_kernel(tc, attn_out, v, x, wo, attn_scale, grad_out, out):
 
         def finish(k):
             j, n, i2, i = place(k)
-            if i2 == 0:
+            if k // 2 not in ress:
                 res = results.tile([P, HEADS_PER_HALF, 2, HD], F32)
                 ress[k // 2] = res
             res = ress[k // 2]
-            for q in range(HEADS_PER_HALF):
-                nc.vector.scalar_tensor_tensor(
-                    out=res[:, q, i2, :],
-                    in0=v_sb[:, 2 * n + q // 2, i, :],
-                    scalar=negcs[k][:, q : q + 1],
-                    in1=gys[k][:, q * HD : (q + 1) * HD],
-                    op0=ALU.mult,
-                    op1=ALU.add,
+            finished.add(k)
+            if k in ON_GPSIMD:
+                correction = work.tile([P, HEADS_PER_HALF, HD], F32)
+                nc.gpsimd.tensor_tensor(
+                    out=correction[:].rearrange("p (h q) d -> p h q d", q=2),
+                    in0=negcs[k][:].rearrange("p (h q) -> p h q", q=2).unsqueeze(3).to_broadcast([P, 2, 2, HD]),
+                    in1=v_sb[:, 2 * n : 2 * n + 2, i, :].unsqueeze(2).to_broadcast([P, 2, 2, HD]),
+                    op=ALU.mult,
                 )
-            if i2 == 1:
-                nc.sync.dma_start(
-                    out=out_view[:, n * HEADS_PER_HALF : (n + 1) * HEADS_PER_HALF, 2 * j : 2 * j + 2, :], in_=res[:]
+                nc.gpsimd.tensor_tensor(
+                    out=res[:, :, i2, :],
+                    in0=correction[:],
+                    in1=gy_copies[k][:].rearrange("p (q d) -> p q d", q=HEADS_PER_HALF),
+                    op=ALU.add,
                 )
+            else:
+                for q in range(HEADS_PER_HALF):
+                    nc.vector.scalar_tensor_tensor(
+                        out=res[:, q, i2, :],
+                        in0=v_sb[:, 2 * n + q // 2, i, :],
+                        scalar=negcs[k][:, q : q + 1],
+                        in1=gys[k][:, q * HD : (q + 1) * HD],
+                        op0=ALU.mult,
+                        op1=ALU.add,
+                    )
+            heads = slice(n * HEADS_PER_HALF, (n + 1) * HEADS_PER_HALF)
+            if k >= UNITS - 2:
+                nc.sync.dma_start(out=out_view[:, heads, i, :], in_=res[:, :, i2, :])
+            elif k ^ 1 in finished:
+                nc.sync.dma_start(out=out_view[:, heads, 2 * j : 2 * j + 2, :], in_=res[:])
 
         ctx.enter_context(tc.manual_schedule())
         transpose_and_scale(0)
@@ -227,26 +247,23 @@ def tile_block_pb_kernel(tc, attn_out, v, x, wo, attn_scale, grad_out, out):
         regroup_wo(nc.vector.tensor_copy, 1, 1)
         quantize_wo(1, 1)
         quantize_wo(1, 0)
+        transpose_and_scale(2)
+        transpose_and_scale(3)
         norms(0)
-        norms(1)
         for k in range(UNITS + FINISH_LAG):
             if k < UNITS:
                 multiply(k)
                 product(k)
-            if k == 1:
-                invert_norms(0)
-            if k in (1, 4, 6):
-                j = max(k // 2, 1)
-                transpose_and_scale(2 * j)
-                transpose_and_scale(2 * j + 1)
-            if k in (2, 5, 7):
-                j = k // 2
-                quantize_gs(j)
-            if k in (4, 7, 10):
-                invert_norms(k // 3)
+            if k in (3, 5, 7, 9):
+                transpose_and_scale({3: 4, 5: 5, 7: 6, 9: 7}[k])
+            if k in (1, 6, 10):
+                quantize_gs({1: 1, 6: 2, 10: 3}[k])
+            if k in (1, 4, 8, 12):
+                invert_norms(k // 4 if k > 1 else 0)
             if DOT_LAG <= k < UNITS + DOT_LAG:
                 dots(k - DOT_LAG)
-            if k in (4, 7):
-                norms(k // 2 if k == 4 else 3)
-            if FINISH_LAG <= k:
-                finish(k - FINISH_LAG)
+            if k in (2, 6, 9):
+                norms({2: 1, 6: 2, 9: 3}[k])
+            for u in range(UNITS):
+                if k == u + (GPSIMD_LAG if u in ON_GPSIMD else FINISH_LAG):
+                    finish(u)

@@ -27,8 +27,7 @@ HEADS_PER_HALF = N // HD
 UNITS = TILES * HALVES
 DOT_LAG = 3
 FINISH_LAG = 4
-GPSIMD_LAG = 3
-ON_GPSIMD = (1, 4, 8)
+ON_GPSIMD = (0, 4, 8)
 
 FLOPS = 2 * T * D * C
 BYTES = 2 * (T * D + D * C + HKV * T * HD + D) + 4 * T * C
@@ -126,28 +125,31 @@ def tile_block_pb_kernel(tc, attn_out, v, x, wo, attn_scale, grad_out, out):
                 in_=wo_grp[:, g, cols, :].rearrange("p c t -> p (c t)"),
             )
 
-        def norms(j):
-            for i in (2 * j, 2 * j + 1):
-                for h in range(HKV):
-                    squares = work.tile([P, HD], BF16)
-                    nc.scalar.activation(
-                        out=squares[:], in_=v_sb[:, h, i, :], func=ACT.Square, accum_out=ss[:, i, h : h + 1]
-                    )
-            pair = slice(2 * j, 2 * j + 2)
+        def squares(i):
+            for h in range(HKV):
+                unread = work.tile([P, HD], BF16)
+                nc.scalar.activation(
+                    out=unread[:], in_=v_sb[:, h, i, :], func=ACT.Square, accum_out=ss[:, i, h : h + 1]
+                )
+
+        def clamp_norms(first, end):
             nc.gpsimd.tensor_scalar(
-                out=clamped[:, pair, :], in0=ss[:, pair, :], scalar1=1e-24, scalar2=-1.0, op0=ALU.max, op1=ALU.mult
+                out=clamped[:, first:end, :],
+                in0=ss[:, first:end, :],
+                scalar1=1e-24,
+                scalar2=-1.0,
+                op0=ALU.max,
+                op1=ALU.mult,
             )
 
-        def invert_norms(j):
-            pair = slice(2 * j, 2 * j + 2)
-            nc.vector.reciprocal(out=nq[:, pair, :], in_=clamped[:, pair, :])
+        def invert_norms(first, end):
+            nc.vector.reciprocal(out=nq[:, first:end, :], in_=clamped[:, first:end, :])
 
         def place(k):
             j, n, i2 = k // 4, k // 2 % 2, k % 2
             return j, n, i2, 2 * j + i2
 
         gys, gy_copies, prods, negcs, ress = {}, {}, {}, {}, {}
-        finished = set()
 
         def multiply(k):
             j, n, i2, i = place(k)
@@ -200,11 +202,10 @@ def tile_block_pb_kernel(tc, attn_out, v, x, wo, attn_scale, grad_out, out):
 
         def finish(k):
             j, n, i2, i = place(k)
-            if k // 2 not in ress:
+            if i2 == 0:
                 res = results.tile([P, HEADS_PER_HALF, 2, HD], F32)
                 ress[k // 2] = res
             res = ress[k // 2]
-            finished.add(k)
             if k in ON_GPSIMD:
                 correction = work.tile([P, HEADS_PER_HALF, HD], F32)
                 nc.gpsimd.tensor_tensor(
@@ -232,7 +233,7 @@ def tile_block_pb_kernel(tc, attn_out, v, x, wo, attn_scale, grad_out, out):
             heads = slice(n * HEADS_PER_HALF, (n + 1) * HEADS_PER_HALF)
             if k >= UNITS - 2:
                 nc.sync.dma_start(out=out_view[:, heads, i, :], in_=res[:, :, i2, :])
-            elif k ^ 1 in finished:
+            elif i2 == 1:
                 nc.sync.dma_start(out=out_view[:, heads, 2 * j : 2 * j + 2, :], in_=res[:])
 
         ctx.enter_context(tc.manual_schedule())
@@ -249,21 +250,29 @@ def tile_block_pb_kernel(tc, attn_out, v, x, wo, attn_scale, grad_out, out):
         quantize_wo(1, 0)
         transpose_and_scale(2)
         transpose_and_scale(3)
-        norms(0)
+        squares(0)
+        squares(1)
+        clamp_norms(0, 2)
+        multiply(0)
+        product(0)
+        quantize_gs(1)
+        transpose_and_scale(4)
+        transpose_and_scale(5)
+        invert_norms(0, 2)
+        for i in range(2, TILES):
+            squares(i)
+        clamp_norms(2, TILES)
+        transpose_and_scale(6)
+        transpose_and_scale(7)
+        quantize_gs(2)
+        quantize_gs(3)
         for k in range(UNITS + FINISH_LAG):
-            if k < UNITS:
+            if 0 < k < UNITS:
                 multiply(k)
                 product(k)
-            if k in (3, 5, 7, 9):
-                transpose_and_scale({3: 4, 5: 5, 7: 6, 9: 7}[k])
-            if k in (1, 6, 10):
-                quantize_gs({1: 1, 6: 2, 10: 3}[k])
-            if k in (1, 4, 8, 12):
-                invert_norms(k // 4 if k > 1 else 0)
+            if k == 1:
+                invert_norms(2, TILES)
             if DOT_LAG <= k < UNITS + DOT_LAG:
                 dots(k - DOT_LAG)
-            if k in (2, 6, 9):
-                norms({2: 1, 6: 2, 9: 3}[k])
-            for u in range(UNITS):
-                if k == u + (GPSIMD_LAG if u in ON_GPSIMD else FINISH_LAG):
-                    finish(u)
+            if k >= FINISH_LAG:
+                finish(k - FINISH_LAG)

@@ -27,7 +27,7 @@ HEADS_PER_HALF = N // HD
 UNITS = TILES * HALVES
 DOT_LAG = 3
 FINISH_LAG = 4
-ON_GPSIMD = (0, 4, 8)
+ON_GPSIMD = (3, 5, 7, 9, 11, 13)
 
 FLOPS = 2 * T * D * C
 BYTES = 2 * (T * D + D * C + HKV * T * HD + D) + 4 * T * C
@@ -46,6 +46,7 @@ def tile_block_pb_kernel(tc, attn_out, v, x, wo, attn_scale, grad_out, out):
         psum = ctx.enter_context(tc.psum_pool(name="psum", bufs=8))
 
         ident = keep.tile([P, P], F32)
+        ident_bf = keep.tile([P, P], BF16)
         sc = keep.tile([P, PASSES, 2, 2], BF16)
         go_sb = keep.tile([P, TILES, D], BF16)
         wo_raw = keep.tile([P, PASSES, 4, C], BF16)
@@ -62,6 +63,7 @@ def tile_block_pb_kernel(tc, attn_out, v, x, wo, attn_scale, grad_out, out):
         warm = keep.tile([P, 1], F32)
 
         masks.make_identity(nc, ident[:])
+        masks.make_identity(nc, ident_bf[:])
         nc.scalar.activation(out=warm[:], in_=ident[:, 0:1], func=ACT.Square)
 
         with nc.allow_non_contiguous_dma(reason="1024 scale values, two to a piece"):
@@ -80,13 +82,18 @@ def tile_block_pb_kernel(tc, attn_out, v, x, wo, attn_scale, grad_out, out):
                 in_=wo[512 * g : 512 * (g + 1), :].rearrange("(u p e) c -> p u (e c)", p=P, e=2),
             )
 
+        def load_v(first, count):
+            tiles = slice(first, first + count)
+            nc.sync.dma_start(out=v_sb[:, :, tiles, :], in_=v_view[:, :, tiles, :])
+
         load_go(0, 1)
         load_go(1, 1)
         load_wo(0)
         load_wo(1)
+        load_v(0, 4)
         load_go(2, 2)
-        nc.sync.dma_start(out=v_sb[:], in_=v_view)
         load_go(4, 2)
+        load_v(4, 4)
         load_go(6, 2)
 
         def transpose_and_scale(i):
@@ -116,6 +123,19 @@ def tile_block_pb_kernel(tc, attn_out, v, x, wo, attn_scale, grad_out, out):
                 out=wo_grp[:, g, cols, :].rearrange("p (c i) t -> p c t i", i=4),
                 in_=wo_raw[:, g, :, cols].rearrange("p t (c i) -> p c t i", i=4),
             )
+
+        def regroup_wo_on_tensor(copy, g, n):
+            for c0 in range(n * N, (n + 1) * N, 2 * P):
+                bank = psum.tile([P, 4 * 2 * P], BF16)
+                for m in range(2):
+                    nc.tensor.matmul(
+                        bank[:, 4 * P * m : 4 * P * (m + 1)],
+                        lhsT=ident_bf[:],
+                        rhs=wo_raw[:, g, :, c0 + P * m : c0 + P * (m + 1)].rearrange("p t c -> p c t"),
+                        start=True,
+                        stop=True,
+                    )
+                copy(out=wo_grp[:, g, c0 : c0 + 2 * P, :].rearrange("p c t -> p (c t)"), in_=bank[:])
 
         def quantize_wo(g, n):
             cols = slice(n * N, (n + 1) * N)
@@ -149,7 +169,7 @@ def tile_block_pb_kernel(tc, attn_out, v, x, wo, attn_scale, grad_out, out):
             j, n, i2 = k // 4, k // 2 % 2, k % 2
             return j, n, i2, 2 * j + i2
 
-        gys, gy_copies, prods, negcs, ress = {}, {}, {}, {}, {}
+        gys, prods, negcs, ress = {}, {}, {}, {}
 
         def multiply(k):
             j, n, i2, i = place(k)
@@ -175,7 +195,6 @@ def tile_block_pb_kernel(tc, attn_out, v, x, wo, attn_scale, grad_out, out):
             if k in ON_GPSIMD:
                 gy_sb = work.tile([P, N], F32)
                 nc.scalar.copy(out=gy_sb[:], in_=gys[k][:])
-                gy_copies[k] = gy_sb
                 nc.gpsimd.tensor_tensor(
                     out=prod_view, in0=gy_sb[:].rearrange("p (h q d) -> p h q d", h=2, q=2), in1=v_pair, op=ALU.mult
                 )
@@ -206,30 +225,15 @@ def tile_block_pb_kernel(tc, attn_out, v, x, wo, attn_scale, grad_out, out):
                 res = results.tile([P, HEADS_PER_HALF, 2, HD], F32)
                 ress[k // 2] = res
             res = ress[k // 2]
-            if k in ON_GPSIMD:
-                correction = work.tile([P, HEADS_PER_HALF, HD], F32)
-                nc.gpsimd.tensor_tensor(
-                    out=correction[:].rearrange("p (h q) d -> p h q d", q=2),
-                    in0=negcs[k][:].rearrange("p (h q) -> p h q", q=2).unsqueeze(3).to_broadcast([P, 2, 2, HD]),
-                    in1=v_sb[:, 2 * n : 2 * n + 2, i, :].unsqueeze(2).to_broadcast([P, 2, 2, HD]),
-                    op=ALU.mult,
+            for q in range(HEADS_PER_HALF):
+                nc.vector.scalar_tensor_tensor(
+                    out=res[:, q, i2, :],
+                    in0=v_sb[:, 2 * n + q // 2, i, :],
+                    scalar=negcs[k][:, q : q + 1],
+                    in1=gys[k][:, q * HD : (q + 1) * HD],
+                    op0=ALU.mult,
+                    op1=ALU.add,
                 )
-                nc.gpsimd.tensor_tensor(
-                    out=res[:, :, i2, :],
-                    in0=correction[:],
-                    in1=gy_copies[k][:].rearrange("p (q d) -> p q d", q=HEADS_PER_HALF),
-                    op=ALU.add,
-                )
-            else:
-                for q in range(HEADS_PER_HALF):
-                    nc.vector.scalar_tensor_tensor(
-                        out=res[:, q, i2, :],
-                        in0=v_sb[:, 2 * n + q // 2, i, :],
-                        scalar=negcs[k][:, q : q + 1],
-                        in1=gys[k][:, q * HD : (q + 1) * HD],
-                        op0=ALU.mult,
-                        op1=ALU.add,
-                    )
             heads = slice(n * HEADS_PER_HALF, (n + 1) * HEADS_PER_HALF)
             if k >= UNITS - 2:
                 nc.sync.dma_start(out=out_view[:, heads, i, :], in_=res[:, :, i2, :])
@@ -240,39 +244,38 @@ def tile_block_pb_kernel(tc, attn_out, v, x, wo, attn_scale, grad_out, out):
         transpose_and_scale(0)
         transpose_and_scale(1)
         quantize_gs(0)
-        regroup_wo(nc.scalar.copy, 0, 0)
+        regroup_wo_on_tensor(nc.scalar.copy, 0, 0)
         regroup_wo(nc.vector.tensor_copy, 0, 1)
         quantize_wo(0, 1)
         quantize_wo(0, 0)
-        regroup_wo(nc.scalar.copy, 1, 0)
+        regroup_wo_on_tensor(nc.scalar.copy, 1, 0)
+        for i in range(4):
+            squares(i)
+        clamp_norms(0, 4)
         regroup_wo(nc.vector.tensor_copy, 1, 1)
         quantize_wo(1, 1)
         quantize_wo(1, 0)
         transpose_and_scale(2)
         transpose_and_scale(3)
-        squares(0)
-        squares(1)
-        clamp_norms(0, 2)
-        multiply(0)
-        product(0)
         quantize_gs(1)
-        transpose_and_scale(4)
-        transpose_and_scale(5)
-        invert_norms(0, 2)
-        for i in range(2, TILES):
-            squares(i)
-        clamp_norms(2, TILES)
-        transpose_and_scale(6)
-        transpose_and_scale(7)
-        quantize_gs(2)
-        quantize_gs(3)
         for k in range(UNITS + FINISH_LAG):
-            if 0 < k < UNITS:
+            if k < UNITS:
                 multiply(k)
                 product(k)
+            if k in (3, 5):
+                transpose_and_scale(k + 1)
+                transpose_and_scale(k + 2)
+            if k in (4, 6):
+                quantize_gs(k // 2)
             if k == 1:
-                invert_norms(2, TILES)
+                invert_norms(0, 4)
+            if k in (6, 8):
+                invert_norms(k - 2, k)
             if DOT_LAG <= k < UNITS + DOT_LAG:
                 dots(k - DOT_LAG)
+            if k in (3, 5):
+                squares(k + 1)
+                squares(k + 2)
+                clamp_norms(k + 1, k + 3)
             if k >= FINISH_LAG:
                 finish(k - FINISH_LAG)

@@ -46,7 +46,6 @@ def tile_block_pb_kernel(tc, attn_out, v, x, wo, attn_scale, grad_out, out):
         psum = ctx.enter_context(tc.psum_pool(name="psum", bufs=8))
 
         ident = keep.tile([P, P], F32)
-        ident_bf = keep.tile([P, P], BF16)
         sc = keep.tile([P, PASSES, 2, 2], BF16)
         go_sb = keep.tile([P, TILES, D], BF16)
         wo_raw = keep.tile([P, PASSES, 4, C], BF16)
@@ -63,7 +62,6 @@ def tile_block_pb_kernel(tc, attn_out, v, x, wo, attn_scale, grad_out, out):
         warm = keep.tile([P, 1], F32)
 
         masks.make_identity(nc, ident[:])
-        masks.make_identity(nc, ident_bf[:])
         nc.scalar.activation(out=warm[:], in_=ident[:, 0:1], func=ACT.Square)
 
         with nc.allow_non_contiguous_dma(reason="1024 scale values, two to a piece"):
@@ -123,19 +121,6 @@ def tile_block_pb_kernel(tc, attn_out, v, x, wo, attn_scale, grad_out, out):
                 out=wo_grp[:, g, cols, :].rearrange("p (c i) t -> p c t i", i=4),
                 in_=wo_raw[:, g, :, cols].rearrange("p t (c i) -> p c t i", i=4),
             )
-
-        def regroup_wo_on_tensor(copy, g, n):
-            for c0 in range(n * N, (n + 1) * N, 2 * P):
-                bank = psum.tile([P, 4 * 2 * P], BF16)
-                for m in range(2):
-                    nc.tensor.matmul(
-                        bank[:, 4 * P * m : 4 * P * (m + 1)],
-                        lhsT=ident_bf[:],
-                        rhs=wo_raw[:, g, :, c0 + P * m : c0 + P * (m + 1)].rearrange("p t c -> p c t"),
-                        start=True,
-                        stop=True,
-                    )
-                copy(out=wo_grp[:, g, c0 : c0 + 2 * P, :].rearrange("p c t -> p (c t)"), in_=bank[:])
 
         def quantize_wo(g, n):
             cols = slice(n * N, (n + 1) * N)
@@ -244,11 +229,11 @@ def tile_block_pb_kernel(tc, attn_out, v, x, wo, attn_scale, grad_out, out):
         transpose_and_scale(0)
         transpose_and_scale(1)
         quantize_gs(0)
-        regroup_wo_on_tensor(nc.scalar.copy, 0, 0)
+        regroup_wo(nc.scalar.copy, 0, 0)
         regroup_wo(nc.vector.tensor_copy, 0, 1)
         quantize_wo(0, 1)
         quantize_wo(0, 0)
-        regroup_wo_on_tensor(nc.scalar.copy, 1, 0)
+        regroup_wo(nc.scalar.copy, 1, 0)
         for i in range(4):
             squares(i)
         clamp_norms(0, 4)

@@ -47,6 +47,7 @@ def tile_block_pb_kernel(tc, attn_out, v, x, wo, attn_scale, grad_out, out):
 
         ident = keep.tile([P, P], F32)
         sc = keep.tile([P, PASSES, 2, 2], BF16)
+        sc_rows = keep.tile([P, 2 * P], BF16)
         go_sb = keep.tile([P, TILES, D], BF16)
         wo_raw = keep.tile([P, PASSES, 4, C], BF16)
         wo_grp = keep.tile([P, PASSES, C, 4], BF16, align_bytes=64)
@@ -64,11 +65,8 @@ def tile_block_pb_kernel(tc, attn_out, v, x, wo, attn_scale, grad_out, out):
         masks.make_identity(nc, ident[:])
         nc.scalar.activation(out=warm[:], in_=ident[:, 0:1], func=ACT.Square)
 
-        with nc.allow_non_contiguous_dma(reason="1024 scale values, two to a piece"):
-            nc.sync.dma_start(
-                out=sc[:].rearrange("p g u e -> p (g u) e"),
-                in_=attn_scale.rearrange("(a p e) -> p a e", p=P, e=2),
-            )
+        nc.vector.memset(sc_rows[:], 0.0)
+        nc.sync.dma_start(out=sc_rows[0:4, :], in_=attn_scale.rearrange("(a c) -> a c", a=4))
 
         def load_go(first, count):
             tiles = slice(first, first + count)
@@ -94,11 +92,19 @@ def tile_block_pb_kernel(tc, attn_out, v, x, wo, attn_scale, grad_out, out):
         load_v(4, 4)
         load_go(6, 2)
 
-        def transpose_and_scale(i):
+        def spread_scale():
+            bank = psum.tile([P, N], F32)
+            nc.tensor.transpose(bank[:, 0:P], sc_rows[:].bitcast(F32), ident[:])
+            nc.vector.tensor_copy(out=sc[:].rearrange("p g u e -> p (g u e)").bitcast(F32), in_=bank[:, 0:4])
+
+        def transpose_go(i):
             go_words = go_sb[:, i, :].bitcast(F32)
             bank = psum.tile([P, N], F32)
             for a in range(4):
                 nc.tensor.transpose(bank[:, a * P : (a + 1) * P], go_words[:, a * P : (a + 1) * P], ident[:])
+            return bank
+
+        def scale(i, bank):
             halves = bank[:].bitcast(BF16).rearrange("p (g u r e) -> p g r u e", g=PASSES, u=2, e=2)
             for g in range(PASSES):
                 nc.vector.tensor_tensor(
@@ -107,6 +113,9 @@ def tile_block_pb_kernel(tc, attn_out, v, x, wo, attn_scale, grad_out, out):
                     in1=sc[:, g].unsqueeze(1).to_broadcast([P, P, 2, 2]),
                     op=ALU.mult,
                 )
+
+        def transpose_and_scale(i):
+            scale(i, transpose_go(i))
 
         def quantize_gs(j):
             nc.vector.quantize_mx(
@@ -226,7 +235,9 @@ def tile_block_pb_kernel(tc, attn_out, v, x, wo, attn_scale, grad_out, out):
                 nc.sync.dma_start(out=out_view[:, heads, 2 * j : 2 * j + 2, :], in_=res[:])
 
         ctx.enter_context(tc.manual_schedule())
-        transpose_and_scale(0)
+        bank = transpose_go(0)
+        spread_scale()
+        scale(0, bank)
         transpose_and_scale(1)
         quantize_gs(0)
         regroup_wo(nc.scalar.copy, 0, 0)

@@ -25,8 +25,8 @@ N = 512
 HALVES = C // N
 HEADS_PER_HALF = N // HD
 UNITS = TILES * HALVES
-DOT_LAG = 3
-FINISH_LAG = 4
+DOT_LAG = 2
+FINISH_LAG = 3
 ON_GPSIMD = (3, 5, 7, 9, 11, 13)
 
 FLOPS = 2 * T * D * C
@@ -82,7 +82,9 @@ def tile_block_pb_kernel(tc, attn_out, v, x, wo, attn_scale, grad_out, out):
             tiles = slice(first, first + count)
             nc.sync.dma_start(out=v_sb[:, :, tiles, :], in_=v_view[:, :, tiles, :])
 
-        load_go(0, 1)
+        for g in range(PASSES):
+            half = slice(512 * g, 512 * (g + 1))
+            nc.sync.dma_start(out=go_sb[:, 0, half], in_=go_view[:, 0, half])
         load_go(1, 1)
         load_wo(0)
         load_wo(1)
@@ -97,16 +99,17 @@ def tile_block_pb_kernel(tc, attn_out, v, x, wo, attn_scale, grad_out, out):
             nc.tensor.transpose(bank[:, 0:P], sc_rows[:].bitcast(F32), ident[:])
             nc.vector.tensor_copy(out=sc[:].rearrange("p g u e -> p (g u e)").bitcast(F32), in_=bank[:, 0:4])
 
-        def transpose_go(i):
+        def transpose_go(i, passes):
             go_words = go_sb[:, i, :].bitcast(F32)
             bank = psum.tile([P, N], F32)
-            for a in range(4):
-                nc.tensor.transpose(bank[:, a * P : (a + 1) * P], go_words[:, a * P : (a + 1) * P], ident[:])
+            for g in passes:
+                for a in (2 * g, 2 * g + 1):
+                    nc.tensor.transpose(bank[:, a * P : (a + 1) * P], go_words[:, a * P : (a + 1) * P], ident[:])
             return bank
 
-        def scale(i, bank):
+        def scale(i, passes, bank):
             halves = bank[:].bitcast(BF16).rearrange("p (g u r e) -> p g r u e", g=PASSES, u=2, e=2)
-            for g in range(PASSES):
+            for g in passes:
                 nc.vector.tensor_tensor(
                     out=gs_grp[:, i, g],
                     in0=halves[:, g],
@@ -115,7 +118,7 @@ def tile_block_pb_kernel(tc, attn_out, v, x, wo, attn_scale, grad_out, out):
                 )
 
         def transpose_and_scale(i):
-            scale(i, transpose_go(i))
+            scale(i, (0, 1), transpose_go(i, (0, 1)))
 
         def quantize_gs(j):
             nc.vector.quantize_mx(
@@ -229,15 +232,16 @@ def tile_block_pb_kernel(tc, attn_out, v, x, wo, attn_scale, grad_out, out):
                     op1=ALU.add,
                 )
             heads = slice(n * HEADS_PER_HALF, (n + 1) * HEADS_PER_HALF)
-            if k >= UNITS - 2:
+            if k >= UNITS - 4:
                 nc.sync.dma_start(out=out_view[:, heads, i, :], in_=res[:, :, i2, :])
             elif i2 == 1:
                 nc.sync.dma_start(out=out_view[:, heads, 2 * j : 2 * j + 2, :], in_=res[:])
 
         ctx.enter_context(tc.manual_schedule())
-        bank = transpose_go(0)
+        bank = transpose_go(0, (0,))
         spread_scale()
-        scale(0, bank)
+        scale(0, (0,), bank)
+        scale(0, (1,), transpose_go(0, (1,)))
         transpose_and_scale(1)
         quantize_gs(0)
         regroup_wo(nc.scalar.copy, 0, 0)
@@ -245,9 +249,10 @@ def tile_block_pb_kernel(tc, attn_out, v, x, wo, attn_scale, grad_out, out):
         quantize_wo(0, 1)
         quantize_wo(0, 0)
         regroup_wo(nc.scalar.copy, 1, 0)
-        for i in range(4):
+        for i in range(6):
             squares(i)
-        clamp_norms(0, 4)
+            if i in (3, 5):
+                clamp_norms(0 if i == 3 else 4, i + 1)
         regroup_wo(nc.vector.tensor_copy, 1, 1)
         quantize_wo(1, 1)
         quantize_wo(1, 0)
@@ -263,15 +268,15 @@ def tile_block_pb_kernel(tc, attn_out, v, x, wo, attn_scale, grad_out, out):
                 transpose_and_scale(k + 2)
             if k in (4, 6):
                 quantize_gs(k // 2)
-            if k == 1:
+            if k == 0:
                 invert_norms(0, 4)
             if k in (6, 8):
                 invert_norms(k - 2, k)
             if DOT_LAG <= k < UNITS + DOT_LAG:
                 dots(k - DOT_LAG)
-            if k in (3, 5):
-                squares(k + 1)
-                squares(k + 2)
-                clamp_norms(k + 1, k + 3)
+            if k == 5:
+                squares(6)
+                squares(7)
+                clamp_norms(6, 8)
             if k >= FINISH_LAG:
                 finish(k - FINISH_LAG)

@@ -112,8 +112,8 @@ def tile_block_pb_kernel(tc, attn_out, v, x, wo, attn_scale, grad_out, out):
             for g in passes:
                 nc.vector.tensor_tensor(
                     out=gs_grp[:, i, g],
-                    in0=halves[:, g],
-                    in1=sc[:, g].unsqueeze(1).to_broadcast([P, P, 2, 2]),
+                    in0=sc[:, g].unsqueeze(1).to_broadcast([P, P, 2, 2]),
+                    in1=halves[:, g],
                     op=ALU.mult,
                 )
 
@@ -197,7 +197,7 @@ def tile_block_pb_kernel(tc, attn_out, v, x, wo, attn_scale, grad_out, out):
                 )
             else:
                 nc.vector.tensor_tensor(
-                    out=prod_view, in0=gys[k][:].rearrange("p (h q d) -> p h q d", h=2, q=2), in1=v_pair, op=ALU.mult
+                    out=prod_view, in0=v_pair, in1=gys[k][:].rearrange("p (h q d) -> p h q d", h=2, q=2), op=ALU.mult
                 )
             prods[k] = prod
 
@@ -242,7 +242,8 @@ def tile_block_pb_kernel(tc, attn_out, v, x, wo, attn_scale, grad_out, out):
         spread_scale()
         scale(0, (0,), bank)
         scale(0, (1,), transpose_go(0, (1,)))
-        transpose_and_scale(1)
+        for g in range(PASSES):
+            scale(1, (g,), transpose_go(1, (g,)))
         quantize_gs(0)
         regroup_wo(nc.scalar.copy, 0, 0)
         regroup_wo(nc.vector.tensor_copy, 0, 1)
@@ -251,8 +252,8 @@ def tile_block_pb_kernel(tc, attn_out, v, x, wo, attn_scale, grad_out, out):
         regroup_wo(nc.scalar.copy, 1, 0)
         for i in range(6):
             squares(i)
-            if i in (3, 5):
-                clamp_norms(0 if i == 3 else 4, i + 1)
+            if i == 3:
+                clamp_norms(0, 4)
         regroup_wo(nc.vector.tensor_copy, 1, 1)
         quantize_wo(1, 1)
         quantize_wo(1, 0)
@@ -270,13 +271,13 @@ def tile_block_pb_kernel(tc, attn_out, v, x, wo, attn_scale, grad_out, out):
                 quantize_gs(k // 2)
             if k == 0:
                 invert_norms(0, 4)
-            if k in (6, 8):
-                invert_norms(k - 2, k)
+            if k == 8:
+                invert_norms(4, 8)
             if DOT_LAG <= k < UNITS + DOT_LAG:
                 dots(k - DOT_LAG)
             if k == 5:
                 squares(6)
                 squares(7)
-                clamp_norms(6, 8)
+                clamp_norms(4, 8)
             if k >= FINISH_LAG:
                 finish(k - FINISH_LAG)

@@ -57,9 +57,9 @@ def tile_block_pb_kernel(tc, attn_out, v, x, wo, attn_scale, grad_out, out):
         gs_codes = keep.tile([P, TILES, PASSES, P], U32, align_bytes=64)
         gs_scales = keep.tile([P, TILES, PASSES, P], U8, align_bytes=64)
         v_sb = keep.tile([P, HKV, TILES, HD], BF16)
-        ss = keep.tile([P, TILES, HKV], F32)
-        clamped = keep.tile([P, TILES, HKV], F32)
-        nq = keep.tile([P, TILES, HKV], F32)
+        ss = keep.tile([P, HALVES, TILES, 2], F32)
+        clamped = keep.tile([P, HALVES, TILES, 2], F32)
+        nq = keep.tile([P, HALVES, TILES, 2], F32)
         warm = keep.tile([P, 1], F32)
 
         masks.make_identity(nc, ident[:])
@@ -78,9 +78,9 @@ def tile_block_pb_kernel(tc, attn_out, v, x, wo, attn_scale, grad_out, out):
                 in_=wo[512 * g : 512 * (g + 1), :].rearrange("(u p e) c -> p u (e c)", p=P, e=2),
             )
 
-        def load_v(first, count):
-            tiles = slice(first, first + count)
-            nc.sync.dma_start(out=v_sb[:, :, tiles, :], in_=v_view[:, :, tiles, :])
+        def load_v(n):
+            heads = slice(2 * n, 2 * n + 2)
+            nc.sync.dma_start(out=v_sb[:, heads], in_=v_view[:, heads])
 
         for g in range(PASSES):
             half = slice(512 * g, 512 * (g + 1))
@@ -88,10 +88,10 @@ def tile_block_pb_kernel(tc, attn_out, v, x, wo, attn_scale, grad_out, out):
         load_go(1, 1)
         load_wo(0)
         load_wo(1)
-        load_v(0, 4)
+        load_v(0)
         load_go(2, 2)
+        load_v(1)
         load_go(4, 2)
-        load_v(4, 4)
         load_go(6, 2)
 
         def spread_scale():
@@ -142,25 +142,27 @@ def tile_block_pb_kernel(tc, attn_out, v, x, wo, attn_scale, grad_out, out):
                 in_=wo_grp[:, g, cols, :].rearrange("p c t -> p (c t)"),
             )
 
-        def squares(i):
-            for h in range(HKV):
-                unread = work.tile([P, HD], BF16)
-                nc.scalar.activation(
-                    out=unread[:], in_=v_sb[:, h, i, :], func=ACT.Square, accum_out=ss[:, i, h : h + 1]
-                )
-
-        def clamp_norms(first, end):
+        def squares(n, first, end):
+            for i in range(first, end):
+                for h2 in range(2):
+                    unread = work.tile([P, HD], BF16)
+                    nc.scalar.activation(
+                        out=unread[:],
+                        in_=v_sb[:, 2 * n + h2, i, :],
+                        func=ACT.Square,
+                        accum_out=ss[:, n, i, h2 : h2 + 1],
+                    )
             nc.gpsimd.tensor_scalar(
-                out=clamped[:, first:end, :],
-                in0=ss[:, first:end, :],
+                out=clamped[:, n, first:end],
+                in0=ss[:, n, first:end],
                 scalar1=1e-24,
                 scalar2=-1.0,
                 op0=ALU.max,
                 op1=ALU.mult,
             )
 
-        def invert_norms(first, end):
-            nc.vector.reciprocal(out=nq[:, first:end, :], in_=clamped[:, first:end, :])
+        def invert_norms(n, first, end):
+            nc.vector.reciprocal(out=nq[:, n, first:end], in_=clamped[:, n, first:end])
 
         def place(k):
             j, n, i2 = k // 4, k // 2 % 2, k % 2
@@ -205,13 +207,12 @@ def tile_block_pb_kernel(tc, attn_out, v, x, wo, attn_scale, grad_out, out):
             j, n, i2, i = place(k)
             negc = work.tile([P, HEADS_PER_HALF], F32)
             for q in range(HEADS_PER_HALF):
-                h = 2 * n + q // 2
                 unread = work.tile([P, HD], BF16)
                 nc.scalar.activation(
                     out=unread[:],
                     in_=prods[k][:, q, :],
                     func=ACT.Copy,
-                    scale=nq[:, i, h : h + 1],
+                    scale=nq[:, n, i, q // 2 : q // 2 + 1],
                     accum_out=negc[:, q : q + 1],
                 )
             negcs[k] = negc
@@ -231,7 +232,12 @@ def tile_block_pb_kernel(tc, attn_out, v, x, wo, attn_scale, grad_out, out):
                     op0=ALU.mult,
                     op1=ALU.add,
                 )
+                if k == UNITS - 1 and q % 2 == 1:
+                    pair = slice(n * HEADS_PER_HALF + q - 1, n * HEADS_PER_HALF + q + 1)
+                    nc.sync.dma_start(out=out_view[:, pair, i, :], in_=res[:, q - 1 : q + 1, i2, :])
             heads = slice(n * HEADS_PER_HALF, (n + 1) * HEADS_PER_HALF)
+            if k == UNITS - 1:
+                return
             if k >= UNITS - 4:
                 nc.sync.dma_start(out=out_view[:, heads, i, :], in_=res[:, :, i2, :])
             elif i2 == 1:
@@ -250,10 +256,8 @@ def tile_block_pb_kernel(tc, attn_out, v, x, wo, attn_scale, grad_out, out):
         quantize_wo(0, 1)
         quantize_wo(0, 0)
         regroup_wo(nc.scalar.copy, 1, 0)
-        for i in range(6):
-            squares(i)
-            if i == 3:
-                clamp_norms(0, 4)
+        squares(0, 0, TILES)
+        squares(1, 0, 4)
         regroup_wo(nc.vector.tensor_copy, 1, 1)
         quantize_wo(1, 1)
         quantize_wo(1, 0)
@@ -270,14 +274,14 @@ def tile_block_pb_kernel(tc, attn_out, v, x, wo, attn_scale, grad_out, out):
             if k in (4, 6):
                 quantize_gs(k // 2)
             if k == 0:
-                invert_norms(0, 4)
+                invert_norms(0, 0, TILES)
+            if k == 2:
+                invert_norms(1, 0, 4)
             if k == 8:
-                invert_norms(4, 8)
+                invert_norms(1, 4, TILES)
             if DOT_LAG <= k < UNITS + DOT_LAG:
                 dots(k - DOT_LAG)
             if k == 5:
-                squares(6)
-                squares(7)
-                clamp_norms(4, 8)
+                squares(1, 4, TILES)
             if k >= FINISH_LAG:
                 finish(k - FINISH_LAG)

@@ -62,11 +62,12 @@ def tile_block_pb_kernel(tc, attn_out, v, x, wo, attn_scale, grad_out, out):
         nq = keep.tile([P, HALVES, TILES, 2], F32)
         warm = keep.tile([P, 1], F32)
 
+        nc.gpsimd.memset(sc_rows[:].bitcast(F32), 0.0)
         masks.make_identity(nc, ident[:])
         nc.scalar.activation(out=warm[:], in_=ident[:, 0:1], func=ACT.Square)
 
-        nc.vector.memset(sc_rows[:], 0.0)
-        nc.sync.dma_start(out=sc_rows[0:4, :], in_=attn_scale.rearrange("(a c) -> a c", a=4))
+        def load_scale():
+            nc.sync.dma_start(out=sc_rows[0:4, :], in_=attn_scale.rearrange("(a c) -> a c", a=4))
 
         def load_go(first, count):
             tiles = slice(first, first + count)
@@ -85,6 +86,7 @@ def tile_block_pb_kernel(tc, attn_out, v, x, wo, attn_scale, grad_out, out):
         for g in range(PASSES):
             half = slice(512 * g, 512 * (g + 1))
             nc.sync.dma_start(out=go_sb[:, 0, half], in_=go_view[:, 0, half])
+        load_scale()
         load_go(1, 1)
         load_wo(0)
         load_wo(1)
@@ -254,20 +256,21 @@ def tile_block_pb_kernel(tc, attn_out, v, x, wo, attn_scale, grad_out, out):
         regroup_wo(nc.scalar.copy, 0, 0)
         regroup_wo(nc.vector.tensor_copy, 0, 1)
         quantize_wo(0, 1)
-        quantize_wo(0, 0)
         regroup_wo(nc.scalar.copy, 1, 0)
         squares(0, 0, TILES)
         squares(1, 0, 4)
         regroup_wo(nc.vector.tensor_copy, 1, 1)
+        quantize_wo(0, 0)
         quantize_wo(1, 1)
         quantize_wo(1, 0)
         transpose_and_scale(2)
         transpose_and_scale(3)
-        quantize_gs(1)
         for k in range(UNITS + FINISH_LAG):
             if k < UNITS:
                 multiply(k)
                 product(k)
+            if k == 0:
+                quantize_gs(1)
             if k in (3, 5):
                 transpose_and_scale(k + 1)
                 transpose_and_scale(k + 2)

@@ -27,7 +27,7 @@ HEADS_PER_HALF = N // HD
 UNITS = TILES * HALVES
 DOT_LAG = 2
 FINISH_LAG = 3
-ON_GPSIMD = (3, 5, 7, 9, 11, 13)
+ON_GPSIMD = tuple(k for k in range(3, UNITS - 1) if k % 3 != 1)
 
 FLOPS = 2 * T * D * C
 BYTES = 2 * (T * D + D * C + HKV * T * HD + D) + 4 * T * C
@@ -79,20 +79,21 @@ def tile_block_pb_kernel(tc, attn_out, v, x, wo, attn_scale, grad_out, out):
                 in_=wo[512 * g : 512 * (g + 1), :].rearrange("(u p e) c -> p u (e c)", p=P, e=2),
             )
 
-        def load_v(n):
-            heads = slice(2 * n, 2 * n + 2)
+        def load_v(first, count):
+            heads = slice(first, first + count)
             nc.sync.dma_start(out=v_sb[:, heads], in_=v_view[:, heads])
 
         for g in range(PASSES):
             half = slice(512 * g, 512 * (g + 1))
             nc.sync.dma_start(out=go_sb[:, 0, half], in_=go_view[:, 0, half])
         load_scale()
+        load_v(0, 1)
         load_go(1, 1)
         load_wo(0)
         load_wo(1)
-        load_v(0)
+        load_v(1, 1)
         load_go(2, 2)
-        load_v(1)
+        load_v(2, 2)
         load_go(4, 2)
         load_go(6, 2)
 
@@ -144,9 +145,9 @@ def tile_block_pb_kernel(tc, attn_out, v, x, wo, attn_scale, grad_out, out):
                 in_=wo_grp[:, g, cols, :].rearrange("p c t -> p (c t)"),
             )
 
-        def squares(n, first, end):
+        def squares(n, first, end, heads=(0, 1)):
             for i in range(first, end):
-                for h2 in range(2):
+                for h2 in heads:
                     unread = work.tile([P, HD], BF16)
                     nc.scalar.activation(
                         out=unread[:],
@@ -154,6 +155,8 @@ def tile_block_pb_kernel(tc, attn_out, v, x, wo, attn_scale, grad_out, out):
                         func=ACT.Square,
                         accum_out=ss[:, n, i, h2 : h2 + 1],
                     )
+
+        def clamp(n, first, end):
             nc.gpsimd.tensor_scalar(
                 out=clamped[:, n, first:end],
                 in0=ss[:, n, first:end],
@@ -253,12 +256,15 @@ def tile_block_pb_kernel(tc, attn_out, v, x, wo, attn_scale, grad_out, out):
         for g in range(PASSES):
             scale(1, (g,), transpose_go(1, (g,)))
         quantize_gs(0)
+        squares(0, 0, TILES, heads=(0,))
         regroup_wo(nc.scalar.copy, 0, 0)
         regroup_wo(nc.vector.tensor_copy, 0, 1)
         quantize_wo(0, 1)
         regroup_wo(nc.scalar.copy, 1, 0)
-        squares(0, 0, TILES)
+        squares(0, 0, TILES, heads=(1,))
+        clamp(0, 0, TILES)
         squares(1, 0, 4)
+        clamp(1, 0, 4)
         regroup_wo(nc.vector.tensor_copy, 1, 1)
         quantize_wo(0, 0)
         quantize_wo(1, 1)
@@ -286,5 +292,6 @@ def tile_block_pb_kernel(tc, attn_out, v, x, wo, attn_scale, grad_out, out):
                 dots(k - DOT_LAG)
             if k == 5:
                 squares(1, 4, TILES)
+                clamp(1, 4, TILES)
             if k >= FINISH_LAG:
                 finish(k - FINISH_LAG)

@@ -25,6 +25,7 @@ N = 512
 HALVES = C // N
 HEADS_PER_HALF = N // HD
 UNITS = TILES * HALVES
+WARM_MATMULS = 5
 DOT_LAG = 2
 FINISH_LAG = 3
 ON_GPSIMD = tuple(k for k in range(3, UNITS - 1) if k % 3 != 1)
@@ -109,6 +110,13 @@ def tile_block_pb_kernel(tc, attn_out, v, x, wo, attn_scale, grad_out, out):
                 for a in (2 * g, 2 * g + 1):
                     nc.tensor.transpose(bank[:, a * P : (a + 1) * P], go_words[:, a * P : (a + 1) * P], ident[:])
             return bank
+
+        def warm_tensor():
+            bank = psum.tile([P, N], F32)
+            for t in range(WARM_MATMULS):
+                nc.tensor.matmul(
+                    bank[:], lhsT=wo_raw[:, 1, t % 4, 0:P], rhs=wo_raw[:, 1, t % 4, 0:N], start=True, stop=True
+                )
 
         def scale(i, passes, bank):
             halves = bank[:].bitcast(BF16).rearrange("p (g u r e) -> p g r u e", g=PASSES, u=2, e=2)
@@ -269,6 +277,7 @@ def tile_block_pb_kernel(tc, attn_out, v, x, wo, attn_scale, grad_out, out):
         quantize_wo(0, 0)
         quantize_wo(1, 1)
         quantize_wo(1, 0)
+        warm_tensor()
         transpose_and_scale(2)
         transpose_and_scale(3)
         for k in range(UNITS + FINISH_LAG):

@@ -28,7 +28,7 @@ UNITS = TILES * HALVES
 WARM_MATMULS = 5
 DOT_LAG = 2
 FINISH_LAG = 3
-ON_GPSIMD = tuple(k for k in range(3, UNITS - 1) if k % 3 != 1)
+ON_GPSIMD = (3, 5, 7, 8, 10, 12, 13)
 
 FLOPS = 2 * T * D * C
 BYTES = 2 * (T * D + D * C + HKV * T * HD + D) + 4 * T * C

@@ -28,7 +28,7 @@ UNITS = TILES * HALVES
 WARM_MATMULS = 5
 DOT_LAG = 2
 FINISH_LAG = 3
-ON_GPSIMD = (3, 5, 7, 8, 10, 12, 13)
+ON_GPSIMD = tuple(k for k in range(3, UNITS - 1) if k % 3 != 1)
 
 FLOPS = 2 * T * D * C
 BYTES = 2 * (T * D + D * C + HKV * T * HD + D) + 4 * T * C
@@ -90,9 +90,9 @@ def tile_block_pb_kernel(tc, attn_out, v, x, wo, attn_scale, grad_out, out):
         load_scale()
         load_v(0, 1)
         load_go(1, 1)
+        load_v(1, 1)
         load_wo(0)
         load_wo(1)
-        load_v(1, 1)
         load_go(2, 2)
         load_v(2, 2)
         load_go(4, 2)
@@ -265,14 +265,14 @@ def tile_block_pb_kernel(tc, attn_out, v, x, wo, attn_scale, grad_out, out):
             scale(1, (g,), transpose_go(1, (g,)))
         quantize_gs(0)
         squares(0, 0, TILES, heads=(0,))
+        squares(0, 0, TILES, heads=(1,))
+        clamp(0, 0, TILES)
         regroup_wo(nc.scalar.copy, 0, 0)
         regroup_wo(nc.vector.tensor_copy, 0, 1)
         quantize_wo(0, 1)
         regroup_wo(nc.scalar.copy, 1, 0)
-        squares(0, 0, TILES, heads=(1,))
-        clamp(0, 0, TILES)
-        squares(1, 0, 4)
-        clamp(1, 0, 4)
+        squares(1, 0, TILES)
+        clamp(1, 0, TILES)
         regroup_wo(nc.vector.tensor_copy, 1, 1)
         quantize_wo(0, 0)
         quantize_wo(1, 1)
@@ -294,13 +294,8 @@ def tile_block_pb_kernel(tc, attn_out, v, x, wo, attn_scale, grad_out, out):
             if k == 0:
                 invert_norms(0, 0, TILES)
             if k == 2:
-                invert_norms(1, 0, 4)
-            if k == 8:
-                invert_norms(1, 4, TILES)
+                invert_norms(1, 0, TILES)
             if DOT_LAG <= k < UNITS + DOT_LAG:
                 dots(k - DOT_LAG)
-            if k == 5:
-                squares(1, 4, TILES)
-                clamp(1, 4, TILES)
             if k >= FINISH_LAG:
                 finish(k - FINISH_LAG)

@@ -28,7 +28,7 @@ UNITS = TILES * HALVES
 WARM_MATMULS = 5
 DOT_LAG = 2
 FINISH_LAG = 3
-ON_GPSIMD = tuple(k for k in range(3, UNITS - 1) if k % 3 != 1)
+ON_GPSIMD = tuple(k for k in range(2, UNITS - 3) if k % 3 != 1)
 
 FLOPS = 2 * T * D * C
 BYTES = 2 * (T * D + D * C + HKV * T * HD + D) + 4 * T * C
@@ -286,11 +286,10 @@ def tile_block_pb_kernel(tc, attn_out, v, x, wo, attn_scale, grad_out, out):
                 product(k)
             if k == 0:
                 quantize_gs(1)
-            if k in (3, 5):
+            if k in (5, 7):
+                quantize_gs((k - 1) // 2)
+            if 3 <= k <= 6:
                 transpose_and_scale(k + 1)
-                transpose_and_scale(k + 2)
-            if k in (4, 6):
-                quantize_gs(k // 2)
             if k == 0:
                 invert_norms(0, 0, TILES)
             if k == 2:

from contextlib import ExitStack

import concourse.masks as masks
import concourse.mybir as mybir

F32 = mybir.dt.float32
BF16 = mybir.dt.bfloat16
U32 = mybir.dt.uint32
U8 = mybir.dt.uint8
E4M3X4 = mybir.dt.float8_e4m3fn_x4
E5M2X4 = mybir.dt.float8_e5m2_x4
ALU = mybir.AluOpType
ACT = mybir.ActivationFunctionType

P = 128
T = 1024
D = 1024
HKV = 4
HD = 128
C = 1024
PASSES = D // 512
TILES = T // P
PAIRS = TILES // 2
N = 512
HALVES = C // N
HEADS_PER_HALF = N // HD
UNITS = TILES * HALVES
WARM_MATMULS = 5
DOT_LAG = 2
FINISH_LAG = 3
ON_GPSIMD = tuple(k for k in range(2, UNITS - 3) if k % 3 != 1)

FLOPS = 2 * T * D * C
BYTES = 2 * (T * D + D * C + HKV * T * HD + D) + 4 * T * C


def tile_block_pb_kernel(tc, attn_out, v, x, wo, attn_scale, grad_out, out):
    nc = tc.nc
    go_view = grad_out.rearrange("b (p i) d -> p (b i) d", i=TILES)
    v_view = v.rearrange("b h (p i) d -> p (b h) i d", i=TILES)
    out_view = out.rearrange("b h g (p i) d -> p (b h g) i d", i=TILES)

    with ExitStack() as ctx:
        keep = ctx.enter_context(tc.tile_pool(name="keep", bufs=1))
        work = ctx.enter_context(tc.tile_pool(name="work", bufs=6))
        results = ctx.enter_context(tc.tile_pool(name="results", bufs=6))
        psum = ctx.enter_context(tc.psum_pool(name="psum", bufs=8))

        ident = keep.tile([P, P], F32)
        sc = keep.tile([P, PASSES, 2, 2], BF16)
        sc_rows = keep.tile([P, 2 * P], BF16)
        go_sb = keep.tile([P, TILES, D], BF16)
        wo_raw = keep.tile([P, PASSES, 4, C], BF16)
        wo_grp = keep.tile([P, PASSES, C, 4], BF16, align_bytes=64)
        wo_codes = keep.tile([P, PASSES, C], U32, align_bytes=64)
        wo_scales = keep.tile([P, PASSES, C], U8, align_bytes=64)
        gs_grp = keep.tile([P, TILES, PASSES, P, 2, 2], BF16, align_bytes=64)
        gs_codes = keep.tile([P, TILES, PASSES, P], U32, align_bytes=64)
        gs_scales = keep.tile([P, TILES, PASSES, P], U8, align_bytes=64)
        v_sb = keep.tile([P, HKV, TILES, HD], BF16)
        ss = keep.tile([P, HALVES, TILES, 2], F32)
        clamped = keep.tile([P, HALVES, TILES, 2], F32)
        nq = keep.tile([P, HALVES, TILES, 2], F32)
        warm = keep.tile([P, 1], F32)

        nc.gpsimd.memset(sc_rows[:].bitcast(F32), 0.0)
        masks.make_identity(nc, ident[:])
        nc.scalar.activation(out=warm[:], in_=ident[:, 0:1], func=ACT.Square)

        def load_scale():
            nc.sync.dma_start(out=sc_rows[0:4, :], in_=attn_scale.rearrange("(a c) -> a c", a=4))

        def load_go(first, count):
            tiles = slice(first, first + count)
            nc.sync.dma_start(out=go_sb[:, tiles, :], in_=go_view[:, tiles, :])

        def load_wo(g):
            nc.sync.dma_start(
                out=wo_raw[:, g].rearrange("p (u e) c -> p u (e c)", e=2),
                in_=wo[512 * g : 512 * (g + 1), :].rearrange("(u p e) c -> p u (e c)", p=P, e=2),
            )

        def load_v(first, count):
            heads = slice(first, first + count)
            nc.sync.dma_start(out=v_sb[:, heads], in_=v_view[:, heads])

        for g in range(PASSES):
            half = slice(512 * g, 512 * (g + 1))
            nc.sync.dma_start(out=go_sb[:, 0, half], in_=go_view[:, 0, half])
        load_scale()
        load_v(0, 1)
        load_go(1, 1)
        load_v(1, 1)
        load_wo(0)
        load_wo(1)
        load_go(2, 2)
        load_v(2, 2)
        load_go(4, 2)
        load_go(6, 2)

        def spread_scale():
            bank = psum.tile([P, N], F32)
            nc.tensor.transpose(bank[:, 0:P], sc_rows[:].bitcast(F32), ident[:])
            nc.vector.tensor_copy(out=sc[:].rearrange("p g u e -> p (g u e)").bitcast(F32), in_=bank[:, 0:4])

        def transpose_go(i, passes):
            go_words = go_sb[:, i, :].bitcast(F32)
            bank = psum.tile([P, N], F32)
            for g in passes:
                for a in (2 * g, 2 * g + 1):
                    nc.tensor.transpose(bank[:, a * P : (a + 1) * P], go_words[:, a * P : (a + 1) * P], ident[:])
            return bank

        def warm_tensor():
            bank = psum.tile([P, N], F32)
            for t in range(WARM_MATMULS):
                nc.tensor.matmul(
                    bank[:], lhsT=wo_raw[:, 1, t % 4, 0:P], rhs=wo_raw[:, 1, t % 4, 0:N], start=True, stop=True
                )

        def scale(i, passes, bank):
            halves = bank[:].bitcast(BF16).rearrange("p (g u r e) -> p g r u e", g=PASSES, u=2, e=2)
            for g in passes:
                nc.vector.tensor_tensor(
                    out=gs_grp[:, i, g],
                    in0=sc[:, g].unsqueeze(1).to_broadcast([P, P, 2, 2]),
                    in1=halves[:, g],
                    op=ALU.mult,
                )

        def transpose_and_scale(i):
            scale(i, (0, 1), transpose_go(i, (0, 1)))

        def quantize_gs(j):
            nc.vector.quantize_mx(
                out=gs_codes[:, 2 * j : 2 * j + 2].rearrange("p i g r -> p (i g r)").bitcast(E5M2X4),
                scales=gs_scales[:, 2 * j : 2 * j + 2].rearrange("p i g r -> p (i g r)"),
                in_=gs_grp[:, 2 * j : 2 * j + 2].rearrange("p i g r u e -> p (i g r u e)"),
            )

        def regroup_wo(copy, g, n):
            cols = slice(n * N, (n + 1) * N)
            copy(
                out=wo_grp[:, g, cols, :].rearrange("p (c i) t -> p c t i", i=4),
                in_=wo_raw[:, g, :, cols].rearrange("p t (c i) -> p c t i", i=4),
            )

        def quantize_wo(g, n):
            cols = slice(n * N, (n + 1) * N)
            nc.vector.quantize_mx(
                out=wo_codes[:, g, cols].bitcast(E4M3X4),
                scales=wo_scales[:, g, cols],
                in_=wo_grp[:, g, cols, :].rearrange("p c t -> p (c t)"),
            )

        def squares(n, first, end, heads=(0, 1)):
            for i in range(first, end):
                for h2 in heads:
                    unread = work.tile([P, HD], BF16)
                    nc.scalar.activation(
                        out=unread[:],
                        in_=v_sb[:, 2 * n + h2, i, :],
                        func=ACT.Square,
                        accum_out=ss[:, n, i, h2 : h2 + 1],
                    )

        def clamp(n, first, end):
            nc.gpsimd.tensor_scalar(
                out=clamped[:, n, first:end],
                in0=ss[:, n, first:end],
                scalar1=1e-24,
                scalar2=-1.0,
                op0=ALU.max,
                op1=ALU.mult,
            )

        def invert_norms(n, first, end):
            nc.vector.reciprocal(out=nq[:, n, first:end], in_=clamped[:, n, first:end])

        def place(k):
            j, n, i2 = k // 4, k // 2 % 2, k % 2
            return j, n, i2, 2 * j + i2

        gys, prods, negcs, ress = {}, {}, {}, {}

        def multiply(k):
            j, n, i2, i = place(k)
            cols = slice(n * N, (n + 1) * N)
            bank = psum.tile([P, N], F32)
            for g in range(PASSES):
                nc.tensor.matmul_mx(
                    out=bank[:],
                    lhsT=gs_codes[:, i, g, :].bitcast(E5M2X4),
                    lhsT_scale=gs_scales[:, i, g, :],
                    rhs=wo_codes[:, g, cols].bitcast(E4M3X4),
                    rhs_scale=wo_scales[:, g, cols],
                    start=(g == 0),
                    stop=(g == PASSES - 1),
                )
            gys[k] = bank

        def product(k):
            j, n, i2, i = place(k)
            v_pair = v_sb[:, 2 * n : 2 * n + 2, i, :].unsqueeze(2).to_broadcast([P, 2, 2, HD])
            prod = work.tile([P, HEADS_PER_HALF, HD], F32)
            prod_view = prod[:].rearrange("p (h q) d -> p h q d", q=2)
            if k in ON_GPSIMD:
                gy_sb = work.tile([P, N], F32)
                nc.scalar.copy(out=gy_sb[:], in_=gys[k][:])
                nc.gpsimd.tensor_tensor(
                    out=prod_view, in0=gy_sb[:].rearrange("p (h q d) -> p h q d", h=2, q=2), in1=v_pair, op=ALU.mult
                )
            else:
                nc.vector.tensor_tensor(
                    out=prod_view, in0=v_pair, in1=gys[k][:].rearrange("p (h q d) -> p h q d", h=2, q=2), op=ALU.mult
                )
            prods[k] = prod

        def dots(k):
            j, n, i2, i = place(k)
            negc = work.tile([P, HEADS_PER_HALF], F32)
            for q in range(HEADS_PER_HALF):
                unread = work.tile([P, HD], BF16)
                nc.scalar.activation(
                    out=unread[:],
                    in_=prods[k][:, q, :],
                    func=ACT.Copy,
                    scale=nq[:, n, i, q // 2 : q // 2 + 1],
                    accum_out=negc[:, q : q + 1],
                )
            negcs[k] = negc

        def finish(k):
            j, n, i2, i = place(k)
            if i2 == 0:
                res = results.tile([P, HEADS_PER_HALF, 2, HD], F32)
                ress[k // 2] = res
            res = ress[k // 2]
            for q in range(HEADS_PER_HALF):
                nc.vector.scalar_tensor_tensor(
                    out=res[:, q, i2, :],
                    in0=v_sb[:, 2 * n + q // 2, i, :],
                    scalar=negcs[k][:, q : q + 1],
                    in1=gys[k][:, q * HD : (q + 1) * HD],
                    op0=ALU.mult,
                    op1=ALU.add,
                )
                if k == UNITS - 1 and q % 2 == 1:
                    pair = slice(n * HEADS_PER_HALF + q - 1, n * HEADS_PER_HALF + q + 1)
                    nc.sync.dma_start(out=out_view[:, pair, i, :], in_=res[:, q - 1 : q + 1, i2, :])
            heads = slice(n * HEADS_PER_HALF, (n + 1) * HEADS_PER_HALF)
            if k == UNITS - 1:
                return
            if k >= UNITS - 4:
                nc.sync.dma_start(out=out_view[:, heads, i, :], in_=res[:, :, i2, :])
            elif i2 == 1:
                nc.sync.dma_start(out=out_view[:, heads, 2 * j : 2 * j + 2, :], in_=res[:])

        ctx.enter_context(tc.manual_schedule())
        bank = transpose_go(0, (0,))
        spread_scale()
        scale(0, (0,), bank)
        scale(0, (1,), transpose_go(0, (1,)))
        for g in range(PASSES):
            scale(1, (g,), transpose_go(1, (g,)))
        quantize_gs(0)
        squares(0, 0, TILES, heads=(0,))
        squares(0, 0, TILES, heads=(1,))
        clamp(0, 0, TILES)
        regroup_wo(nc.scalar.copy, 0, 0)
        regroup_wo(nc.vector.tensor_copy, 0, 1)
        quantize_wo(0, 1)
        regroup_wo(nc.scalar.copy, 1, 0)
        squares(1, 0, TILES)
        clamp(1, 0, TILES)
        regroup_wo(nc.vector.tensor_copy, 1, 1)
        quantize_wo(0, 0)
        quantize_wo(1, 1)
        quantize_wo(1, 0)
        warm_tensor()
        transpose_and_scale(2)
        transpose_and_scale(3)
        for k in range(UNITS + FINISH_LAG):
            if k < UNITS:
                multiply(k)
                product(k)
            if k == 0:
                quantize_gs(1)
            if k in (5, 7):
                quantize_gs((k - 1) // 2)
            if 3 <= k <= 6:
                transpose_and_scale(k + 1)
            if k == 0:
                invert_norms(0, 0, TILES)
            if k == 2:
                invert_norms(1, 0, TILES)
            if DOT_LAG <= k < UNITS + DOT_LAG:
                dots(k - DOT_LAG)
            if k >= FINISH_LAG:
                finish(k - FINISH_LAG)
